import numpy as np
import ml_dtypes

BF16 = ml_dtypes.bfloat16


def bf(x):
    return np.asarray(x, np.float32).astype(BF16)


def f32(x):
    return np.asarray(x, np.float32)


def f64(x):
    return np.asarray(x).astype(np.float64)


def striped(idx):
    return np.tile(idx.reshape(-1, 16).T, (8, 1))


C, S, N, DK = 256, 4096, 2048, 256


def setup_inputs():
    return {"base": f32(np.random.standard_normal((C, S))), "x_own": bf(np.random.standard_normal((DK, N))), "x_ring": bf(np.random.standard_normal((DK, N))), "w_own": bf(np.random.standard_normal((DK, C)) / np.sqrt(DK)), "w_ring": bf(np.random.standard_normal((DK, C)) / np.sqrt(DK)), "bias": f32(0.1 * np.random.standard_normal((C, 1))), "offs": striped(np.random.permutation(S)[:N])}


def reference(base, x_own, x_ring, w_own, w_ring, bias, offs):
    idx = offs[:16].T.reshape(-1)
    out = f64(base).copy()
    out[:, idx] = (f64(w_own).T @ f64(x_own) + f64(bias)) + f64(w_ring).T @ f64(x_ring)
    return out

@@ -1,0 +1,67 @@
+import concourse.mybir as mybir
+
+FLOPS = 2 * 256 * 2048 * (256 + 256)
+
+P = 128
+BANK = 512
+
+BF16, F32, U16 = mybir.dt.bfloat16, mybir.dt.float32, mybir.dt.uint16
+ADD = mybir.AluOpType.add
+IDENTITY = mybir.ActivationFunctionType.Identity
+
+
+def tile_tpasyncdense_kernel(tc, base, x_own, x_ring, w_own, w_ring, bias, offs, out):
+    nc = tc.nc
+    n_features, n_slots = base.shape
+    n_shard, n_tokens = x_own.shape
+    feature_blocks = n_features // P
+    k_tiles = n_shard // P
+    chunks = n_tokens // BANK
+
+    with (
+        tc.tile_pool(name="held", bufs=1) as held,
+        tc.psum_pool(name="psum", bufs=8) as psum,
+    ):
+        offsets = held.tile([P, n_tokens // 16], U16, name="offsets")
+        nc.sync.dma_start(offsets[:], offs)
+
+        shards = []
+        for label, w_dram, x_dram in (("own", w_own, x_own), ("ring", w_ring, x_ring)):
+            w_tile = held.tile([P, k_tiles, n_features], BF16, name=f"w_{label}")
+            x_tile = held.tile([P, k_tiles, n_tokens], BF16, name=f"x_{label}")
+            nc.sync.dma_start(w_tile[:], w_dram.rearrange("(kt p) c -> p kt c", p=P))
+            nc.sync.dma_start(x_tile[:], x_dram.rearrange("(kt p) n -> p kt n", p=P))
+            shards.append((label, w_tile, x_tile))
+
+        windows, biases = [], []
+        for b in range(feature_blocks):
+            rows = slice(b * P, (b + 1) * P)
+            bias_tile = held.tile([P, 1], F32, name=f"bias{b}")
+            nc.scalar.dma_start(bias_tile[:], bias[rows, :])
+            biases.append(bias_tile)
+            window = held.tile([P, n_slots], F32, name=f"window{b}")
+            nc.sync.dma_start(window[:], base[rows, :])
+            windows.append(window)
+
+        for b in range(feature_blocks):
+            rows = slice(b * P, (b + 1) * P)
+            partial = {}
+            for label, w_tile, x_tile in shards:
+                partial[label] = held.tile([P, n_tokens], F32, name=f"{label}_part{b}")
+                for q in range(chunks):
+                    cols = slice(q * BANK, (q + 1) * BANK)
+                    acc = psum.tile([P, BANK], F32, name="acc")
+                    for kt in range(k_tiles):
+                        nc.tensor.matmul(
+                            acc[:], w_tile[:, kt, rows], x_tile[:, kt, cols],
+                            start=(kt == 0), stop=(kt == k_tiles - 1),
+                        )
+                    if label == "own":
+                        nc.scalar.activation(partial[label][:, cols], acc[:], IDENTITY, bias=biases[b][:])
+                    else:
+                        nc.scalar.activation(partial[label][:, cols], acc[:], IDENTITY)
+
+            nc.vector.tensor_tensor(
+                windows[b][:].indirect(offsets[:]), partial["own"][:], partial["ring"][:], ADD
+            )
+            nc.sync.dma_start(out[rows, :], windows[b][:])

@@ -22,16 +22,19 @@ def tile_tpasyncdense_kernel(tc, base, x_own, x_ring, w_own, w_ring, bias, offs,
         tc.tile_pool(name="held", bufs=1) as held,
         tc.psum_pool(name="psum", bufs=8) as psum,
     ):
-        offsets = held.tile([P, n_tokens // 16], U16, name="offsets")
-        nc.sync.dma_start(offsets[:], offs)
-
         shards = []
         for label, w_dram, x_dram in (("own", w_own, x_own), ("ring", w_ring, x_ring)):
             w_tile = held.tile([P, k_tiles, n_features], BF16, name=f"w_{label}")
             x_tile = held.tile([P, k_tiles, n_tokens], BF16, name=f"x_{label}")
-            nc.sync.dma_start(w_tile[:], w_dram.rearrange("(kt p) c -> p kt c", p=P))
-            nc.sync.dma_start(x_tile[:], x_dram.rearrange("(kt p) n -> p kt n", p=P))
+            nc.scalar.dma_start(w_tile[:], w_dram.rearrange("(kt p) c -> p kt c", p=P))
+            x_rows = x_dram.rearrange("(kt p) n -> p kt n", p=P)
+            for q in range(chunks):
+                cols = slice(q * BANK, (q + 1) * BANK)
+                nc.sync.dma_start(x_tile[:, :, cols], x_rows[:, :, cols])
             shards.append((label, w_tile, x_tile))
+
+        offsets = held.tile([P, n_tokens // 16], U16, name="offsets")
+        nc.sync.dma_start(offsets[:], offs)
 
         windows, biases = [], []
         for b in range(feature_blocks):

@@ -22,19 +22,16 @@ def tile_tpasyncdense_kernel(tc, base, x_own, x_ring, w_own, w_ring, bias, offs,
         tc.tile_pool(name="held", bufs=1) as held,
         tc.psum_pool(name="psum", bufs=8) as psum,
     ):
+        offsets = held.tile([P, n_tokens // 16], U16, name="offsets")
+        nc.sync.dma_start(offsets[:], offs)
+
         shards = []
         for label, w_dram, x_dram in (("own", w_own, x_own), ("ring", w_ring, x_ring)):
             w_tile = held.tile([P, k_tiles, n_features], BF16, name=f"w_{label}")
             x_tile = held.tile([P, k_tiles, n_tokens], BF16, name=f"x_{label}")
             nc.scalar.dma_start(w_tile[:], w_dram.rearrange("(kt p) c -> p kt c", p=P))
-            x_rows = x_dram.rearrange("(kt p) n -> p kt n", p=P)
-            for q in range(chunks):
-                cols = slice(q * BANK, (q + 1) * BANK)
-                nc.sync.dma_start(x_tile[:, :, cols], x_rows[:, :, cols])
+            nc.sync.dma_start(x_tile[:], x_dram.rearrange("(kt p) n -> p kt n", p=P))
             shards.append((label, w_tile, x_tile))
-
-        offsets = held.tile([P, n_tokens // 16], U16, name="offsets")
-        nc.sync.dma_start(offsets[:], offs)
 
         windows, biases = [], []
         for b in range(feature_blocks):

@@ -58,6 +58,8 @@ def tile_tpasyncdense_kernel(tc, base, x_own, x_ring, w_own, w_ring, bias, offs,
                         )
                     if label == "own":
                         nc.scalar.activation(partial[label][:, cols], acc[:], IDENTITY, bias=biases[b][:])
+                    elif b == 0:
+                        nc.vector.tensor_copy(partial[label][:, cols], acc[:])
                     else:
                         nc.scalar.activation(partial[label][:, cols], acc[:], IDENTITY)
 

@@ -28,10 +28,13 @@ def tile_tpasyncdense_kernel(tc, base, x_own, x_ring, w_own, w_ring, bias, offs,
         shards = []
         for label, w_dram, x_dram in (("own", w_own, x_own), ("ring", w_ring, x_ring)):
             w_tile = held.tile([P, k_tiles, n_features], BF16, name=f"w_{label}")
-            x_tile = held.tile([P, k_tiles, n_tokens], BF16, name=f"x_{label}")
             nc.scalar.dma_start(w_tile[:], w_dram.rearrange("(kt p) c -> p kt c", p=P))
-            nc.sync.dma_start(x_tile[:], x_dram.rearrange("(kt p) n -> p kt n", p=P))
-            shards.append((label, w_tile, x_tile))
+            x_tiles = []
+            for kt in range(k_tiles):
+                x_tile = held.tile([P, n_tokens], BF16, name=f"x_{label}{kt}")
+                nc.sync.dma_start(x_tile[:], x_dram[kt * P : (kt + 1) * P, :])
+                x_tiles.append(x_tile)
+            shards.append((label, w_tile, x_tiles))
 
         windows, biases = [], []
         for b in range(feature_blocks):
@@ -46,16 +49,18 @@ def tile_tpasyncdense_kernel(tc, base, x_own, x_ring, w_own, w_ring, bias, offs,
         for b in range(feature_blocks):
             rows = slice(b * P, (b + 1) * P)
             partial = {}
-            for label, w_tile, x_tile in shards:
+            for label, w_tile, x_tiles in shards:
                 partial[label] = held.tile([P, n_tokens], F32, name=f"{label}_part{b}")
-                for q in range(chunks):
-                    cols = slice(q * BANK, (q + 1) * BANK)
-                    acc = psum.tile([P, BANK], F32, name="acc")
-                    for kt in range(k_tiles):
+                accs = [psum.tile([P, BANK], F32, name="acc") for q in range(chunks)]
+                for kt in range(k_tiles):
+                    for q in range(chunks):
                         nc.tensor.matmul(
-                            acc[:], w_tile[:, kt, rows], x_tile[:, kt, cols],
+                            accs[q][:], w_tile[:, kt, rows], x_tiles[kt][:, q * BANK : (q + 1) * BANK],
                             start=(kt == 0), stop=(kt == k_tiles - 1),
                         )
+                for q in range(chunks):
+                    cols = slice(q * BANK, (q + 1) * BANK)
+                    acc = accs[q]
                     if label == "own":
                         nc.scalar.activation(partial[label][:, cols], acc[:], IDENTITY, bias=biases[b][:])
                     elif b == 0:

@@ -71,4 +71,6 @@ def tile_tpasyncdense_kernel(tc, base, x_own, x_ring, w_own, w_ring, bias, offs,
             nc.vector.tensor_tensor(
                 windows[b][:].indirect(offsets[:]), partial["own"][:], partial["ring"][:], ADD
             )
-            nc.sync.dma_start(out[rows, :], windows[b][:])
+            half = n_slots // 2
+            nc.sync.dma_start(out[rows, :half], windows[b][:, :half])
+            nc.scalar.dma_start(out[rows, half:], windows[b][:, half:])

@@ -28,11 +28,12 @@ def tile_tpasyncdense_kernel(tc, base, x_own, x_ring, w_own, w_ring, bias, offs,
         shards = []
         for label, w_dram, x_dram in (("own", w_own, x_own), ("ring", w_ring, x_ring)):
             w_tile = held.tile([P, k_tiles, n_features], BF16, name=f"w_{label}")
-            nc.scalar.dma_start(w_tile[:], w_dram.rearrange("(kt p) c -> p kt c", p=P))
+            nc.scalar.dma_start(w_tile[:], w_dram.rearrange("(p kt) c -> p kt c", p=P))
+            x_rows = x_dram.rearrange("(p kt) n -> p kt n", p=P)
             x_tiles = []
             for kt in range(k_tiles):
                 x_tile = held.tile([P, n_tokens], BF16, name=f"x_{label}{kt}")
-                nc.sync.dma_start(x_tile[:], x_dram[kt * P : (kt + 1) * P, :])
+                nc.sync.dma_start(x_tile[:], x_rows[:, kt, :])
                 x_tiles.append(x_tile)
             shards.append((label, w_tile, x_tiles))
 
@@ -40,7 +41,8 @@ def tile_tpasyncdense_kernel(tc, base, x_own, x_ring, w_own, w_ring, bias, offs,
         for b in range(feature_blocks):
             rows = slice(b * P, (b + 1) * P)
             bias_tile = held.tile([P, 1], F32, name=f"bias{b}")
-            nc.scalar.dma_start(bias_tile[:], bias[rows, :])
+            bias_queue = nc.scalar if b == 0 else nc.sync
+            bias_queue.dma_start(bias_tile[:], bias[rows, :])
             biases.append(bias_tile)
             window = held.tile([P, n_slots], F32, name=f"window{b}")
             nc.sync.dma_start(window[:], base[rows, :])
@@ -71,6 +73,4 @@ def tile_tpasyncdense_kernel(tc, base, x_own, x_ring, w_own, w_ring, bias, offs,
             nc.vector.tensor_tensor(
                 windows[b][:].indirect(offsets[:]), partial["own"][:], partial["ring"][:], ADD
             )
-            half = n_slots // 2
-            nc.sync.dma_start(out[rows, :half], windows[b][:, :half])
-            nc.scalar.dma_start(out[rows, half:], windows[b][:, half:])
+            nc.sync.dma_start(out[rows, :], windows[b][:])

@@ -25,24 +25,23 @@ def tile_tpasyncdense_kernel(tc, base, x_own, x_ring, w_own, w_ring, bias, offs,
         offsets = held.tile([P, n_tokens // 16], U16, name="offsets")
         nc.sync.dma_start(offsets[:], offs)
 
-        shards = []
-        for label, w_dram, x_dram in (("own", w_own, x_own), ("ring", w_ring, x_ring)):
-            w_tile = held.tile([P, k_tiles, n_features], BF16, name=f"w_{label}")
-            nc.scalar.dma_start(w_tile[:], w_dram.rearrange("(p kt) c -> p kt c", p=P))
+        inputs = (("own", w_own, x_own), ("ring", w_ring, x_ring))
+        x_tiles = {}
+        for label, w_dram, x_dram in inputs:
             x_rows = x_dram.rearrange("(p kt) n -> p kt n", p=P)
-            x_tiles = []
             for kt in range(k_tiles):
-                x_tile = held.tile([P, n_tokens], BF16, name=f"x_{label}{kt}")
-                nc.sync.dma_start(x_tile[:], x_rows[:, kt, :])
-                x_tiles.append(x_tile)
-            shards.append((label, w_tile, x_tiles))
+                x_tiles[label, kt] = held.tile([P, n_tokens], BF16, name=f"x_{label}{kt}")
+                nc.sync.dma_start(x_tiles[label, kt][:], x_rows[:, kt, :])
 
-        windows, biases = [], []
+        weights, biases, windows = {}, [], []
         for b in range(feature_blocks):
             rows = slice(b * P, (b + 1) * P)
+            small_queue = nc.scalar if b == 0 else nc.sync
+            for label, w_dram, x_dram in inputs:
+                weights[label, b] = held.tile([P, k_tiles, P], BF16, name=f"w_{label}{b}")
+                small_queue.dma_start(weights[label, b][:], w_dram.rearrange("(p kt) c -> p kt c", p=P)[:, :, rows])
             bias_tile = held.tile([P, 1], F32, name=f"bias{b}")
-            bias_queue = nc.scalar if b == 0 else nc.sync
-            bias_queue.dma_start(bias_tile[:], bias[rows, :])
+            small_queue.dma_start(bias_tile[:], bias[rows, :])
             biases.append(bias_tile)
             window = held.tile([P, n_slots], F32, name=f"window{b}")
             nc.sync.dma_start(window[:], base[rows, :])
@@ -51,13 +50,13 @@ def tile_tpasyncdense_kernel(tc, base, x_own, x_ring, w_own, w_ring, bias, offs,
         for b in range(feature_blocks):
             rows = slice(b * P, (b + 1) * P)
             partial = {}
-            for label, w_tile, x_tiles in shards:
+            for label in ("own", "ring"):
                 partial[label] = held.tile([P, n_tokens], F32, name=f"{label}_part{b}")
                 accs = [psum.tile([P, BANK], F32, name="acc") for q in range(chunks)]
                 for kt in range(k_tiles):
                     for q in range(chunks):
                         nc.tensor.matmul(
-                            accs[q][:], w_tile[:, kt, rows], x_tiles[kt][:, q * BANK : (q + 1) * BANK],
+                            accs[q][:], weights[label, b][:, kt, :], x_tiles[label, kt][:, q * BANK : (q + 1) * BANK],
                             start=(kt == 0), stop=(kt == k_tiles - 1),
                         )
                 for q in range(chunks):

import concourse.mybir as mybir

FLOPS = 2 * 256 * 2048 * (256 + 256)

P = 128
BANK = 512

BF16, F32, U16 = mybir.dt.bfloat16, mybir.dt.float32, mybir.dt.uint16
ADD = mybir.AluOpType.add
IDENTITY = mybir.ActivationFunctionType.Identity


def tile_tpasyncdense_kernel(tc, base, x_own, x_ring, w_own, w_ring, bias, offs, out):
    nc = tc.nc
    n_features, n_slots = base.shape
    n_shard, n_tokens = x_own.shape
    feature_blocks = n_features // P
    k_tiles = n_shard // P
    chunks = n_tokens // BANK

    with (
        tc.tile_pool(name="held", bufs=1) as held,
        tc.psum_pool(name="psum", bufs=8) as psum,
    ):
        offsets = held.tile([P, n_tokens // 16], U16, name="offsets")
        nc.sync.dma_start(offsets[:], offs)

        inputs = (("own", w_own, x_own), ("ring", w_ring, x_ring))
        x_tiles = {}
        for label, w_dram, x_dram in inputs:
            x_rows = x_dram.rearrange("(p kt) n -> p kt n", p=P)
            for kt in range(k_tiles):
                x_tiles[label, kt] = held.tile([P, n_tokens], BF16, name=f"x_{label}{kt}")
                nc.sync.dma_start(x_tiles[label, kt][:], x_rows[:, kt, :])

        weights, biases, windows = {}, [], []
        for b in range(feature_blocks):
            rows = slice(b * P, (b + 1) * P)
            small_queue = nc.scalar if b == 0 else nc.sync
            for label, w_dram, x_dram in inputs:
                weights[label, b] = held.tile([P, k_tiles, P], BF16, name=f"w_{label}{b}")
                small_queue.dma_start(weights[label, b][:], w_dram.rearrange("(p kt) c -> p kt c", p=P)[:, :, rows])
            bias_tile = held.tile([P, 1], F32, name=f"bias{b}")
            small_queue.dma_start(bias_tile[:], bias[rows, :])
            biases.append(bias_tile)
            window = held.tile([P, n_slots], F32, name=f"window{b}")
            nc.sync.dma_start(window[:], base[rows, :])
            windows.append(window)

        for b in range(feature_blocks):
            rows = slice(b * P, (b + 1) * P)
            partial = {}
            for label in ("own", "ring"):
                partial[label] = held.tile([P, n_tokens], F32, name=f"{label}_part{b}")
                accs = [psum.tile([P, BANK], F32, name="acc") for q in range(chunks)]
                for kt in range(k_tiles):
                    for q in range(chunks):
                        nc.tensor.matmul(
                            accs[q][:], weights[label, b][:, kt, :], x_tiles[label, kt][:, q * BANK : (q + 1) * BANK],
                            start=(kt == 0), stop=(kt == k_tiles - 1),
                        )
                for q in range(chunks):
                    cols = slice(q * BANK, (q + 1) * BANK)
                    acc = accs[q]
                    if label == "own":
                        nc.scalar.activation(partial[label][:, cols], acc[:], IDENTITY, bias=biases[b][:])
                    elif b == 0:
                        nc.vector.tensor_copy(partial[label][:, cols], acc[:])
                    else:
                        nc.scalar.activation(partial[label][:, cols], acc[:], IDENTITY)

            nc.vector.tensor_tensor(
                windows[b][:].indirect(offsets[:]), partial["own"][:], partial["ring"][:], ADD
            )
            nc.sync.dma_start(out[rows, :], windows[b][:])
